import numpy as np
import ml_dtypes


def mxq(x, axis, fmt="e4m3"):
    dtype, down = {"e4m3": (ml_dtypes.float8_e4m3fn, 7), "e5m2": (ml_dtypes.float8_e5m2, 14)}[fmt]
    v = np.moveaxis(np.asarray(x, np.float32).astype(ml_dtypes.bfloat16).astype(np.float64), axis, -1)
    blocks = v.reshape(v.shape[:-1] + (-1, 32))
    amax = np.abs(blocks).max(-1, keepdims=True)
    byte = np.maximum(np.where(amax > 0, np.frexp(amax)[1] - 1 + 127, 0) - down, 1)
    scale = np.exp2(byte - 127.0)
    codes = (blocks / scale).astype(np.float32).astype(dtype).astype(np.float64)
    return np.moveaxis((codes * scale).reshape(v.shape), -1, axis)


WIDE = False


def mx_kscale(k):
    if not WIDE:
        return np.ones(k)
    levels = np.array([10, -10, 5, -5, 0])
    if k % 512:
        return np.exp2(np.random.permutation(np.resize(levels, k // 32))).repeat(32)
    a = np.empty((k // 512, 16))
    for p in range(k // 512):
        a[p, :8] = np.random.permutation(np.resize(levels, 8))
        for g in range(8):
            far = levels[np.abs(levels - a[p, g]) >= 10]
            a[p, g + 8] = far[np.random.randint(len(far))]
    return np.exp2(a.ravel()).repeat(32)


BF16 = ml_dtypes.bfloat16


def bf(x):
    return np.asarray(x, np.float32).astype(BF16)


def f64(x):
    return np.asarray(x).astype(np.float64)


E2M1 = np.array([0.0, 0.5, 1.0, 1.5, 2.0, 3.0, 4.0, 6.0, -0.0, -0.5, -1.0, -1.5, -2.0, -3.0, -4.0, -6.0])


def pack_weight(w, fmt):
    k, n = w.shape
    w = f64(bf(w)).reshape(k // 32, 32, n)
    amax = np.abs(w).max(1)
    if fmt == "e4m3":
        byte = np.frexp(amax)[1] - 1 + 127 - 7
    else:
        mant, ex = np.frexp(amax / 6.0)
        byte = np.where(mant > 0.5, ex, ex - 1) + 127
    byte = np.clip(np.where(amax > 0, byte, 1), 1, 254)
    scaled = (w * np.exp2(127.0 - byte)[:, None, :]).reshape(k, n).astype(np.float32)
    by_word = np.ascontiguousarray(scaled.reshape(k // 512, 128, 4, n).transpose(0, 1, 3, 2))
    if fmt == "e4m3":
        words = by_word.astype(ml_dtypes.float8_e4m3fn).view(np.uint8)
    else:
        c = by_word.astype(ml_dtypes.float4_e2m1fn).view(np.uint8) & 0xF
        words = c[..., 0::2] | (c[..., 1::2] << 4)
    return np.ascontiguousarray(words), np.ascontiguousarray(byte.astype(np.uint8).reshape(k // 512, 16, n))


def unpack_weight(words, scales, fmt):
    g, p, n, _ = words.shape
    if fmt == "e4m3":
        vals = np.ascontiguousarray(words).view(ml_dtypes.float8_e4m3fn).astype(np.float64)
    else:
        nib = np.empty((g, p, n, 4), np.uint8)
        nib[..., 0::2] = words & 0xF
        nib[..., 1::2] = words >> 4
        vals = E2M1[nib]
    vals = vals * np.repeat(np.exp2(scales.astype(np.float64) - 127.0), 8, axis=1)[..., None]
    return vals.transpose(0, 1, 3, 2).reshape(g * 512, n)


N, T, H, P0, P1, C0, NC, V0, V1 = 2, 256, 2048, 512, 128, 20000, 2, 8192, 12288


def draw0():
    s, t = mx_kscale(H), mx_kscale(P0)
    x = bf(np.random.standard_normal((N, T, H)) * s)
    tail_proj_0_words, tail_proj_0_scales = pack_weight(np.random.standard_normal((H, P0)) / np.sqrt(H) / s[:, None] * t, "e4m3")
    tail_w_0_words, tail_w_0_scales = pack_weight(np.random.standard_normal((P0, V0)) * 2.0 / np.sqrt(P0) / t[:, None], "e4m3")
    return {"x": x,
            "tail_proj_0_words": tail_proj_0_words,
            "tail_proj_0_scales": tail_proj_0_scales,
            "tail_w_0_words": tail_w_0_words,
            "tail_w_0_scales": tail_w_0_scales,
            "cluster_prob": bf(0.05 + 0.55 * np.random.random((N, T))[..., None])}


def core(x, tail_proj_0_words, tail_proj_0_scales, tail_w_0_words, tail_w_0_scales, cluster_prob):
    h = mxq(f64(x), 2, "e4m3") @ unpack_weight(tail_proj_0_words, tail_proj_0_scales, "e4m3")
    logits = mxq(h, 2, "e4m3") @ unpack_weight(tail_w_0_words, tail_w_0_scales, "e4m3")
    e = np.exp(logits - logits.max(-1, keepdims=True))
    return e / e.sum(-1, keepdims=True) * f64(cluster_prob)


def e4m3fn_bytes(y):
    return np.clip(np.asarray(y, np.float64), -448.0, 448.0).astype(np.float32).astype(ml_dtypes.float8_e4m3fn).view(np.uint8)


def e4m3fn_values(b):
    return np.asarray(b, np.uint8).view(ml_dtypes.float8_e4m3fn).astype(np.float64)


def setup_inputs():
    d = draw0()
    x0 = np.asarray(d['x']).astype(np.float64)
    s = (np.max(np.abs(x0), axis=(0, 1), keepdims=True) / 448.0).astype(np.float32)
    out = {}
    for k, v in d.items():
        if k == 'x':
            out['x_bytes'] = e4m3fn_bytes(x0 / s.astype(np.float64))
            out['x_scale'] = s
        else:
            out[k] = v
    return out


def reference(x_bytes, x_scale, tail_proj_0_words, tail_proj_0_scales, tail_w_0_words, tail_w_0_scales, cluster_prob):
    return core(e4m3fn_values(x_bytes) * x_scale.astype(np.float64), tail_proj_0_words, tail_proj_0_scales, tail_w_0_words, tail_w_0_scales, cluster_prob)

@@ -1,0 +1,365 @@
+from contextlib import ExitStack
+
+import concourse.mybir as mybir
+from concourse.masks import make_identity
+
+F32 = mybir.dt.float32
+BF16 = mybir.dt.bfloat16
+I32 = mybir.dt.int32
+U32 = mybir.dt.uint32
+U8 = mybir.dt.uint8
+FP8 = mybir.dt.float8_e4m3fn
+FP8X4 = mybir.dt.float8_e4m3fn_x4
+ALU = mybir.AluOpType
+ACT = mybir.ActivationFunctionType
+AX = mybir.AxisListType
+
+P = 128
+TILES = 4
+K1 = 2048
+G1 = K1 // 512
+K2 = 512
+VOC = 8192
+BANK = 512
+NB = VOC // BANK
+LEAD = 4
+
+FLOPS = 2 * 512 * K1 * K2 + 2 * 512 * K2 * VOC
+
+
+def tile_adaptiveinputsoftmax_pa_w8_kernel(
+    tc, x_bytes, x_scale, w1_words, w1_scales, w2_words, w2_scales, cluster_prob, out
+):
+    nc = tc.nc
+    xb_hbm = x_bytes.rearrange("a b k -> (a b) k").rearrange("(p i) k -> p i k", i=TILES)
+    xs_hbm = x_scale.rearrange("a b k -> (a b k)").rearrange("(g p t) -> p g t", p=P, t=4)
+    cp_hbm = cluster_prob.rearrange("a b o -> (a b o)").rearrange("(p i) -> p i", i=TILES)
+    out_hbm = out.rearrange("a b v -> (a b) v").rearrange("(p i) v -> p i v", i=TILES)
+    w1s_hbm = w1_scales.bitcast(I32)
+    w2s_hbm = w2_scales[0].bitcast(I32)
+    w2w_hbm = w2_words[0].rearrange("p n t -> p (n t)").bitcast(I32)
+
+    with ExitStack() as ctx:
+        keep = ctx.enter_context(tc.tile_pool(name="keep", bufs=1))
+        work = ctx.enter_context(tc.tile_pool(name="work", bufs=2))
+        big = ctx.enter_context(tc.tile_pool(name="big", bufs=4))
+        psum = ctx.enter_context(tc.psum_pool(name="psum", bufs=1))
+        ctx.enter_context(tc.manual_schedule())
+
+        warm = keep.tile([P, 1], F32)
+        nc.vector.memset(warm[:], 0.0)
+        warm_out = keep.tile([P, 1], F32)
+        nc.scalar.activation(out=warm_out[:], in_=warm[:], func=ACT.Exp)
+        ident = keep.tile([P, P], F32)
+        make_identity(nc, ident[:])
+
+        w1s = keep.tile([P, K2], U8, align_bytes=64)
+        nc.vector.memset(w1s[:].bitcast(I32), 0)
+        w2s = keep.tile([P, VOC // 4], U8, align_bytes=64)
+        nc.vector.memset(w2s[:].bitcast(I32), 0)
+
+        x8 = keep.tile([P, TILES, K1], U8, align_bytes=64)
+        xs = keep.tile([P, G1, 4], F32)
+        cp16 = keep.tile([P, TILES], BF16)
+        w1w = keep.tile([P, G1, K2], I32, align_bytes=64)
+        w2w = keep.tile([P, VOC], I32, align_bytes=64)
+
+        def load_x(i):
+            nc.sync.dma_start(out=x8[:, i, :], in_=xb_hbm[:, i, :])
+
+        def load_w2(c):
+            nc.sync.dma_start(out=w2w[:, c * 1024:(c + 1) * 1024], in_=w2w_hbm[:, c * 1024:(c + 1) * 1024])
+
+        load_x(0)
+        nc.sync.dma_start(out=xs[:], in_=xs_hbm)
+        nc.sync.dma_start(out=cp16[:], in_=cp_hbm)
+        for q in range(4):
+            nc.sync.dma_start(
+                out=w1s[32 * q:32 * q + 16, :].bitcast(I32), in_=w1s_hbm[:, 4 * q:4 * q + 4, :]
+            )
+        load_x(1)
+        for g in range(G1):
+            nc.sync.dma_start(out=w1w[:, g, :], in_=w1_words[g].rearrange("p n t -> p (n t)").bitcast(I32))
+        for q in range(4):
+            nc.sync.dma_start(
+                out=w2s[32 * q:32 * q + 16, :].bitcast(I32),
+                in_=w2s_hbm[4 * q:4 * q + 4, :].rearrange("i (j c) -> j i c", j=4),
+            )
+        load_w2(0)
+        load_w2(1)
+        load_x(2)
+        load_w2(2)
+        load_w2(3)
+        load_x(3)
+        for c in range(4, 8):
+            load_w2(c)
+        cp = keep.tile([P, TILES], F32)
+
+        xb = [keep.tile([P, K1], BF16, name=f"xb{i}", align_bytes=64) for i in range(TILES)]
+        xg = [keep.tile([P, K1], BF16, name=f"xg{i}", align_bytes=64) for i in range(TILES)]
+        xq = [keep.tile([P, G1 * P], U32, name=f"xq{i}", align_bytes=64) for i in range(TILES)]
+        xqs = [keep.tile([P, G1 * P], U8, name=f"xqs{i}", align_bytes=64) for i in range(TILES)]
+        hb = [keep.tile([P, K2], BF16, name=f"hb{i}", align_bytes=64) for i in range(TILES)]
+        hg = [keep.tile([P, K2], BF16, name=f"hg{i}", align_bytes=64) for i in range(TILES)]
+        hq = [keep.tile([P, P], U32, name=f"hq{i}", align_bytes=64) for i in range(TILES)]
+        hqs = [keep.tile([P, P], U8, name=f"hqs{i}", align_bytes=64) for i in range(TILES)]
+        xt = {}
+        hp = {}
+
+        def cast(i, half, engine):
+            cols = slice(half * 1024, (half + 1) * 1024)
+            src = x8[:, i, cols].bitcast(FP8)
+            if engine == "s":
+                nc.scalar.copy(out=xb[i][:, cols], in_=src)
+            elif engine == "v":
+                nc.vector.tensor_copy(out=xb[i][:, cols], in_=src)
+            else:
+                nc.gpsimd.tensor_copy(out=xb[i][:, cols], in_=src)
+
+        def flip_x(i, half):
+            t = psum.tile([P, 4, P], F32, name="xt", bufs=2)
+            words = xb[i][:].bitcast(F32)
+            for j in range(4):
+                g = 2 * half + j // 2
+                u = j % 2
+                nc.tensor.transpose(t[:, j, :], words[:, 256 * g + u:256 * (g + 1):2], ident[:])
+            xt[i, half] = t
+
+        def product(i, g):
+            t = xt[i, g // 2]
+            j = 2 * (g % 2)
+            src = t[:, j:j + 2, :].bitcast(BF16).rearrange("p u (r e) -> p r u e", e=2)
+            dst = xg[i][:, 512 * g:512 * (g + 1)].rearrange("p (r u e) -> p r u e", u=2, e=2)
+            sc = xs[:, g, :].rearrange("p (u e) -> p u e", e=2).unsqueeze(1).to_broadcast([P, P, 2, 2])
+            nc.vector.tensor_tensor(out=dst, in0=src, in1=sc, op=ALU.mult)
+
+        def quant_x(i, half):
+            nc.vector.quantize_mx(
+                out=xq[i][:, 256 * half:256 * (half + 1)].bitcast(FP8X4),
+                scales=xqs[i][:, 256 * half:256 * (half + 1)],
+                in_=xg[i][:, 1024 * half:1024 * (half + 1)],
+            )
+
+        def mm_h(i):
+            t = psum.tile([P, K2], F32, name="hp", bufs=1)
+            for g in range(G1):
+                nc.tensor.matmul_mx(
+                    out=t[:],
+                    lhsT=xq[i][:, P * g:P * (g + 1)].bitcast(FP8X4),
+                    lhsT_scale=xqs[i][:, P * g:P * (g + 1)],
+                    rhs=w1w[:, g, :].bitcast(FP8X4),
+                    rhs_scale=w1s[4 * g:P, :],
+                    start=(g == 0),
+                    stop=(g == G1 - 1),
+                )
+            hp[i] = t
+
+        def copy_h(i):
+            nc.scalar.copy(out=hb[i][:], in_=hp[i][:])
+
+        def flip_h(i):
+            t = psum.tile([P, 2, P], F32, name="xt", bufs=2)
+            words = hb[i][:].bitcast(F32)
+            for u in range(2):
+                nc.tensor.transpose(t[:, u, :], words[:, u::2], ident[:])
+            xt[i, "h"] = t
+
+        def copy_hg(i):
+            nc.scalar.copy(
+                out=hg[i][:].bitcast(F32).rearrange("p (r u) -> p r u", u=2),
+                in_=xt[i, "h"][:].rearrange("p u r -> p r u"),
+            )
+
+        def quant_h(i):
+            nc.vector.quantize_mx(out=hq[i][:].bitcast(FP8X4), scales=hqs[i][:], in_=hg[i][:])
+
+        e = {}
+        nm = {}
+        ss = {}
+        fg = {}
+        lg = {}
+
+        def mm_l(s):
+            if s >= TILES * NB:
+                return
+            i, b = divmod(s, NB)
+            t = psum.tile([P, BANK], F32, name="lg", bufs=5)
+            cols = slice(b * BANK, (b + 1) * BANK)
+            quarter, rest = divmod(b, 4)
+            nc.tensor.matmul_mx(
+                out=t[:],
+                lhsT=hq[i][:].bitcast(FP8X4),
+                lhsT_scale=hqs[i][:],
+                rhs=w2w[:, cols].bitcast(FP8X4),
+                rhs_scale=w2s[4 * quarter:P, rest * BANK:(rest + 1) * BANK],
+                start=True,
+                stop=True,
+            )
+            lg[s] = t
+
+        def reduce(s):
+            i, b = divmod(s, NB)
+            if b == 0:
+                nm[i] = work.tile([P, NB], F32, name="nm")
+                ss[i] = work.tile([P, NB], F32, name="ss")
+                e[i] = big.tile([P, VOC], F32, name="e")
+            nc.vector.tensor_reduce(out=nm[i][:, b:b + 1], in_=lg[s][:], axis=AX.X, op=ALU.max, negate=True)
+
+        def expo(s):
+            i, b = divmod(s, NB)
+            nc.scalar.activation(
+                out=e[i][:, b * BANK:(b + 1) * BANK],
+                in_=lg[s][:],
+                func=ACT.Exp,
+                bias=nm[i][:, b:b + 1],
+                scale=1.0,
+                accum_out=ss[i][:, b:b + 1],
+            )
+
+        fin = {}
+
+        def fin_max(i):
+            t = work.tile([P, 1], F32, name="negm")
+            nc.vector.tensor_reduce(out=t[:], in_=nm[i][:], axis=AX.X, op=ALU.min)
+            f = work.tile([P, NB], F32, name="f")
+            nc.scalar.activation(out=f[:], in_=nm[i][:], func=ACT.Exp, bias=t[:], scale=-1.0)
+            fin[i] = f
+
+        def fin_sum(i):
+            prod = work.tile([P, NB], F32, name="prod")
+            total = work.tile([P, 1], F32, name="total")
+            nc.vector.scalar_tensor_tensor(
+                out=prod[:], in0=fin[i][:], scalar=1.0, in1=ss[i][:], op0=ALU.mult, op1=ALU.mult,
+                accum_out=total[:],
+            )
+            fin[i, "t"] = total
+
+        def fin_rec(i):
+            r = work.tile([P, 1], F32, name="r")
+            nc.vector.reciprocal(out=r[:], in_=fin[i, "t"][:])
+            fin[i, "r"] = r
+
+        def fin_fg(i):
+            fg[i] = work.tile([P, NB], F32, name="fg")
+            nc.vector.tensor_scalar(
+                out=fg[i][:], in0=fin[i][:], scalar1=fin[i, "r"][:], scalar2=cp[:, i:i + 1],
+                op0=ALU.mult, op1=ALU.mult,
+            )
+
+        def scale(i, b, engine):
+            part = e[i][:, b * BANK:(b + 1) * BANK]
+            f = fg[i][:, b:b + 1]
+            if engine == "g":
+                nc.gpsimd.tensor_scalar(out=part, in0=part, scalar1=f, scalar2=1.0, op0=ALU.mult, op1=ALU.mult)
+            elif engine == "v":
+                nc.vector.tensor_scalar(out=part, in0=part, scalar1=f, scalar2=None, op0=ALU.mult)
+            else:
+                nc.scalar.activation(out=part, in_=part, func=ACT.Copy, scale=f)
+
+        def store(i, b0, b1):
+            cols = slice(b0 * BANK, b1 * BANK)
+            nc.sync.dma_start(out=out_hbm[:, i, cols], in_=e[i][:, cols])
+
+        def scale_all(i):
+            for q in range(4):
+                for b in range(4 * q, 4 * q + 4):
+                    scale(i, b, "v" if i == 2 and b % 4 == 3 else "g")
+                store(i, 4 * q, 4 * q + 4)
+
+        cast(0, 0, "v")
+        cast(0, 1, "s")
+        flip_x(0, 0)
+        flip_x(0, 1)
+        cast(1, 0, "s")
+        cast(1, 1, "s")
+        nc.vector.tensor_copy(out=cp[:], in_=cp16[:])
+        for g in range(4):
+            product(0, g)
+        quant_x(0, 0)
+        quant_x(0, 1)
+        flip_x(1, 0)
+        mm_h(0)
+        flip_x(1, 1)
+        copy_h(0)
+        flip_h(0)
+        product(1, 0)
+        product(1, 1)
+        copy_hg(0)
+        quant_h(0)
+        for s in range(LEAD):
+            mm_l(s)
+        for half in range(2):
+            cast(2, half, "g")
+        for half in range(2):
+            cast(3, half, "g")
+
+        extras = {}
+
+        def at(i, b, fn, *args):
+            extras.setdefault((i, b), []).append((fn, args))
+
+        at(0, 0, product, 1, 2)
+        at(0, 1, product, 1, 3)
+        at(0, 2, quant_x, 1, 0)
+        at(0, 3, quant_x, 1, 1)
+        at(0, 3, mm_h, 1)
+        at(0, 4, copy_h, 1)
+        at(0, 4, flip_h, 1)
+        at(0, 5, copy_hg, 1)
+        at(0, 6, quant_h, 1)
+        at(0, 8, flip_x, 2, 0)
+        at(0, 10, product, 2, 0)
+        at(0, 12, product, 2, 1)
+        at(0, 12, flip_x, 2, 1)
+        at(0, 14, quant_x, 2, 0)
+        at(1, 0, product, 2, 2)
+        at(1, 2, product, 2, 3)
+        at(1, 3, quant_x, 2, 1)
+        at(1, 4, mm_h, 2)
+        at(1, 5, copy_h, 2)
+        at(1, 5, flip_h, 2)
+        at(1, 6, copy_hg, 2)
+        at(1, 8, quant_h, 2)
+        at(1, 8, flip_x, 3, 0)
+        at(1, 10, product, 3, 0)
+        at(1, 12, product, 3, 1)
+        at(1, 12, flip_x, 3, 1)
+        at(1, 14, quant_x, 3, 0)
+        at(2, 0, product, 3, 2)
+        at(2, 2, product, 3, 3)
+        at(2, 3, quant_x, 3, 1)
+        at(2, 4, mm_h, 3)
+        at(2, 5, copy_h, 3)
+        at(2, 5, flip_h, 3)
+        at(2, 6, copy_hg, 3)
+        at(2, 8, quant_h, 3)
+        for i in range(1, TILES):
+            at(i, 0, fin_max, i - 1)
+            at(i, 1, fin_sum, i - 1)
+            at(i, 2, fin_rec, i - 1)
+            at(i, 3, fin_fg, i - 1)
+            at(i, 3, scale_all, i - 1)
+
+        for s in range(TILES * NB):
+            reduce(s)
+            expo(s)
+            mm_l(s + LEAD)
+            for fn, args in extras.get(divmod(s, NB), []):
+                fn(*args)
+
+        last = TILES - 1
+        fin_max(last)
+        fin_sum(last)
+        fin_rec(last)
+        fin_fg(last)
+        scale(last, 0, "v")
+        scale(last, 1, "s")
+        store(last, 0, 1)
+        store(last, 1, 2)
+        scale(last, 2, "v")
+        scale(last, 3, "v")
+        store(last, 2, 4)
+        for q in range(1, 4):
+            for b in range(4 * q, 4 * q + 4):
+                scale(last, b, "v")
+            store(last, 4 * q, 4 * q + 4)

@@ -22,7 +22,9 @@ K2 = 512
 VOC = 8192
 BANK = 512
 NB = VOC // BANK
-LEAD = 4
+LAG = 2
+LEAD = 5 - LAG
+SCALERS = ['ggggggggsgggggsg', 'gggggggggggggggs', 'sgggggsggvgvggvg', 'vsvsvvssssvvvsvs']
 
 FLOPS = 2 * 512 * K1 * K2 + 2 * 512 * K2 * VOC
 
@@ -72,14 +74,17 @@ def tile_adaptiveinputsoftmax_pa_w8_kernel(
 
         load_x(0)
         nc.sync.dma_start(out=xs[:], in_=xs_hbm)
-        nc.sync.dma_start(out=cp16[:], in_=cp_hbm)
         for q in range(4):
             nc.sync.dma_start(
                 out=w1s[32 * q:32 * q + 16, :].bitcast(I32), in_=w1s_hbm[:, 4 * q:4 * q + 4, :]
             )
         load_x(1)
-        for g in range(G1):
-            nc.sync.dma_start(out=w1w[:, g, :], in_=w1_words[g].rearrange("p n t -> p (n t)").bitcast(I32))
+        for g in range(0, G1, 2):
+            nc.sync.dma_start(
+                out=w1w[:, g:g + 2, :],
+                in_=w1_words[g:g + 2].rearrange("g p n t -> p g (n t)").bitcast(I32),
+            )
+            load_x(2 + g // 2)
         for q in range(4):
             nc.sync.dma_start(
                 out=w2s[32 * q:32 * q + 16, :].bitcast(I32),
@@ -87,16 +92,21 @@ def tile_adaptiveinputsoftmax_pa_w8_kernel(
             )
         load_w2(0)
         load_w2(1)
-        load_x(2)
         load_w2(2)
+        nc.sync.dma_start(out=cp16[:], in_=cp_hbm)
         load_w2(3)
-        load_x(3)
         for c in range(4, 8):
             load_w2(c)
         cp = keep.tile([P, TILES], F32)
 
         xb = [keep.tile([P, K1], BF16, name=f"xb{i}", align_bytes=64) for i in range(TILES)]
-        xg = [keep.tile([P, K1], BF16, name=f"xg{i}", align_bytes=64) for i in range(TILES)]
+        xg = {}
+
+        def xg_tile(i):
+            if i not in xg:
+                xg[i] = keep.tile([P, K1], BF16, name=f"xg{i % 2}", align_bytes=64)
+            return xg[i]
+
         xq = [keep.tile([P, G1 * P], U32, name=f"xq{i}", align_bytes=64) for i in range(TILES)]
         xqs = [keep.tile([P, G1 * P], U8, name=f"xqs{i}", align_bytes=64) for i in range(TILES)]
         hb = [keep.tile([P, K2], BF16, name=f"hb{i}", align_bytes=64) for i in range(TILES)]
@@ -117,7 +127,10 @@ def tile_adaptiveinputsoftmax_pa_w8_kernel(
                 nc.gpsimd.tensor_copy(out=xb[i][:, cols], in_=src)
 
         def flip_x(i, half):
-            t = psum.tile([P, 4, P], F32, name="xt", bufs=2)
+            if i < 2:
+                t = psum.tile([P, 4, P], F32, name="lg", bufs=5)
+            else:
+                t = psum.tile([P, 4, P], F32, name="xt", bufs=2)
             words = xb[i][:].bitcast(F32)
             for j in range(4):
                 g = 2 * half + j // 2
@@ -129,16 +142,12 @@ def tile_adaptiveinputsoftmax_pa_w8_kernel(
             t = xt[i, g // 2]
             j = 2 * (g % 2)
             src = t[:, j:j + 2, :].bitcast(BF16).rearrange("p u (r e) -> p r u e", e=2)
-            dst = xg[i][:, 512 * g:512 * (g + 1)].rearrange("p (r u e) -> p r u e", u=2, e=2)
+            dst = xg_tile(i)[:, 512 * g:512 * (g + 1)].rearrange("p (r u e) -> p r u e", u=2, e=2)
             sc = xs[:, g, :].rearrange("p (u e) -> p u e", e=2).unsqueeze(1).to_broadcast([P, P, 2, 2])
             nc.vector.tensor_tensor(out=dst, in0=src, in1=sc, op=ALU.mult)
 
-        def quant_x(i, half):
-            nc.vector.quantize_mx(
-                out=xq[i][:, 256 * half:256 * (half + 1)].bitcast(FP8X4),
-                scales=xqs[i][:, 256 * half:256 * (half + 1)],
-                in_=xg[i][:, 1024 * half:1024 * (half + 1)],
-            )
+        def quant_x(i):
+            nc.vector.quantize_mx(out=xq[i][:].bitcast(FP8X4), scales=xqs[i][:], in_=xg_tile(i)[:])
 
         def mm_h(i):
             t = psum.tile([P, K2], F32, name="hp", bufs=1)
@@ -154,8 +163,11 @@ def tile_adaptiveinputsoftmax_pa_w8_kernel(
                 )
             hp[i] = t
 
-        def copy_h(i):
-            nc.scalar.copy(out=hb[i][:], in_=hp[i][:])
+        def copy_h(i, engine="s"):
+            if engine == "s":
+                nc.scalar.copy(out=hb[i][:], in_=hp[i][:])
+            else:
+                nc.vector.tensor_copy(out=hb[i][:], in_=hp[i][:])
 
         def flip_h(i):
             t = psum.tile([P, 2, P], F32, name="xt", bufs=2)
@@ -164,11 +176,13 @@ def tile_adaptiveinputsoftmax_pa_w8_kernel(
                 nc.tensor.transpose(t[:, u, :], words[:, u::2], ident[:])
             xt[i, "h"] = t
 
-        def copy_hg(i):
-            nc.scalar.copy(
-                out=hg[i][:].bitcast(F32).rearrange("p (r u) -> p r u", u=2),
-                in_=xt[i, "h"][:].rearrange("p u r -> p r u"),
-            )
+        def copy_hg(i, engine="s"):
+            dst = hg[i][:].bitcast(F32).rearrange("p (r u) -> p r u", u=2)
+            src = xt[i, "h"][:].rearrange("p u r -> p r u")
+            if engine == "s":
+                nc.scalar.copy(out=dst, in_=src)
+            else:
+                nc.vector.tensor_copy(out=dst, in_=src)
 
         def quant_h(i):
             nc.vector.quantize_mx(out=hq[i][:].bitcast(FP8X4), scales=hqs[i][:], in_=hg[i][:])
@@ -177,6 +191,7 @@ def tile_adaptiveinputsoftmax_pa_w8_kernel(
         nm = {}
         ss = {}
         fg = {}
+        fc = {}
         lg = {}
 
         def mm_l(s):
@@ -221,9 +236,15 @@ def tile_adaptiveinputsoftmax_pa_w8_kernel(
         def fin_max(i):
             t = work.tile([P, 1], F32, name="negm")
             nc.vector.tensor_reduce(out=t[:], in_=nm[i][:], axis=AX.X, op=ALU.min)
+            fin[i, "m"] = t
+
+        def fin_f(i):
+            t = fin[i, "m"]
             f = work.tile([P, NB], F32, name="f")
             nc.scalar.activation(out=f[:], in_=nm[i][:], func=ACT.Exp, bias=t[:], scale=-1.0)
             fin[i] = f
+            fc[i] = work.tile([P, NB], F32, name="fc")
+            nc.scalar.activation(out=fc[i][:], in_=f[:], func=ACT.Copy, scale=cp[:, i:i + 1])
 
         def fin_sum(i):
             prod = work.tile([P, NB], F32, name="prod")
@@ -240,126 +261,87 @@ def tile_adaptiveinputsoftmax_pa_w8_kernel(
             fin[i, "r"] = r
 
         def fin_fg(i):
+            if not any(c in "sSg" for c in SCALERS[i]):
+                return
             fg[i] = work.tile([P, NB], F32, name="fg")
-            nc.vector.tensor_scalar(
-                out=fg[i][:], in0=fin[i][:], scalar1=fin[i, "r"][:], scalar2=cp[:, i:i + 1],
-                op0=ALU.mult, op1=ALU.mult,
-            )
+            nc.scalar.activation(out=fg[i][:], in_=fc[i][:], func=ACT.Copy, scale=fin[i, "r"][:])
 
         def scale(i, b, engine):
             part = e[i][:, b * BANK:(b + 1) * BANK]
-            f = fg[i][:, b:b + 1]
-            if engine == "g":
-                nc.gpsimd.tensor_scalar(out=part, in0=part, scalar1=f, scalar2=1.0, op0=ALU.mult, op1=ALU.mult)
-            elif engine == "v":
-                nc.vector.tensor_scalar(out=part, in0=part, scalar1=f, scalar2=None, op0=ALU.mult)
+            if engine == "s":
+                nc.scalar.activation(out=part, in_=part, func=ACT.Copy, scale=fg[i][:, b:b + 1])
+            elif engine == "g":
+                nc.gpsimd.tensor_scalar(
+                    out=part, in0=part, scalar1=fg[i][:, b:b + 1], scalar2=1.0, op0=ALU.mult, op1=ALU.mult
+                )
             else:
-                nc.scalar.activation(out=part, in_=part, func=ACT.Copy, scale=f)
+                nc.vector.tensor_scalar(
+                    out=part, in0=part, scalar1=fc[i][:, b:b + 1], scalar2=fin[i, "r"][:], op0=ALU.mult, op1=ALU.mult
+                )
 
         def store(i, b0, b1):
             cols = slice(b0 * BANK, b1 * BANK)
             nc.sync.dma_start(out=out_hbm[:, i, cols], in_=e[i][:, cols])
 
-        def scale_all(i):
-            for q in range(4):
-                for b in range(4 * q, 4 * q + 4):
-                    scale(i, b, "v" if i == 2 and b % 4 == 3 else "g")
-                store(i, 4 * q, 4 * q + 4)
+        def cast_cp():
+            nc.vector.tensor_copy(out=cp[:], in_=cp16[:])
+
+        def scale_group(i, q):
+            for b in range(4 * q, 4 * q + 4):
+                scale(i, b, SCALERS[i][b])
+            store(i, 4 * q, 4 * q + 4)
 
         cast(0, 0, "v")
         cast(0, 1, "s")
         flip_x(0, 0)
         flip_x(0, 1)
-        cast(1, 0, "s")
-        cast(1, 1, "s")
-        nc.vector.tensor_copy(out=cp[:], in_=cp16[:])
         for g in range(4):
             product(0, g)
-        quant_x(0, 0)
-        quant_x(0, 1)
+        cast(1, 0, "s")
+        cast(1, 1, "s")
         flip_x(1, 0)
-        mm_h(0)
         flip_x(1, 1)
+        quant_x(0)
+        mm_h(0)
+        cast(2, 0, "s")
+        cast(2, 1, "s")
+        for g in range(4):
+            product(1, g)
         copy_h(0)
         flip_h(0)
-        product(1, 0)
-        product(1, 1)
         copy_hg(0)
         quant_h(0)
         for s in range(LEAD):
             mm_l(s)
-        for half in range(2):
-            cast(2, half, "g")
-        for half in range(2):
-            cast(3, half, "g")
-
+        plan = [(1, 'flip_x', 2, 0), (3, 'quant_x', 1), (4, 'cast', 3, 1, 's'), (4, 'product', 2, 0), (5, 'flip_x', 2, 1), (5, 'mm_h', 1), (6, 'product', 2, 2), (7, 'cast_cp'), (7, 'copy_h', 1, 's'), (7, 'product', 2, 3), (7, 'flip_h', 1), (9, 'product', 2, 1), (10, 'quant_x', 2), (10, 'copy_hg', 1, 's'), (10, 'mm_h', 2), (11, 'quant_h', 1), (12, 'cast', 3, 0, 's'), (13, 'flip_x', 3, 0), (15, 'copy_h', 2, 's'), (17, 'product', 3, 0), (18, 'fin_sum', 0), (19, 'flip_h', 2), (19, 'fin_rec', 0), (19, 'fin_fg', 0), (19, 'scale', 0, 0, 'g'), (19, 'scale', 0, 1, 'g'), (19, 'store', 0, 0, 2), (20, 'copy_hg', 2, 's'), (20, 'scale', 0, 2, 'g'), (20, 'scale', 0, 3, 'g'), (20, 'store', 0, 2, 4), (21, 'scale', 0, 4, 'g'), (22, 'scale', 0, 5, 'g'), (22, 'scale', 0, 6, 'g'), (23, 'flip_x', 3, 1), (23, 'quant_h', 2), (23, 'scale', 0, 7, 'g'), (23, 'store', 0, 4, 8), (23, 'scale', 0, 8, 's'), (24, 'scale', 0, 9, 'g'), (25, 'scale', 0, 10, 'g'), (25, 'scale', 0, 11, 'g'), (25, 'store', 0, 8, 12), (26, 'product', 3, 1), (26, 'scale', 0, 12, 'g'), (26, 'scale', 0, 13, 'g'), (27, 'product', 3, 2), (27, 'product', 3, 3), (27, 'scale', 0, 14, 's'), (28, 'scale', 0, 15, 'g'), (28, 'store', 0, 12, 16), (34, 'quant_x', 3), (34, 'mm_h', 3), (34, 'fin_sum', 1), (35, 'fin_rec', 1), (35, 'fin_fg', 1), (35, 'scale', 1, 0, 'g'), (35, 'scale', 1, 1, 'g'), (36, 'scale', 1, 2, 'g'), (36, 'scale', 1, 3, 'g'), (36, 'store', 1, 0, 4), (37, 'scale', 1, 4, 'g'), (38, 'copy_h', 3, 'v'), (38, 'scale', 1, 5, 'g'), (38, 'scale', 1, 6, 'g'), (39, 'flip_h', 3), (39, 'scale', 1, 7, 'g'), (39, 'store', 1, 4, 8), (39, 'scale', 1, 8, 'g'), (40, 'scale', 1, 9, 'g'), (41, 'scale', 1, 10, 'g'), (41, 'scale', 1, 11, 'g'), (41, 'store', 1, 8, 12), (42, 'scale', 1, 12, 'g'), (42, 'scale', 1, 13, 'g'), (43, 'copy_hg', 3, 's'), (43, 'scale', 1, 14, 'g'), (44, 'quant_h', 3), (44, 'scale', 1, 15, 's'), (44, 'store', 1, 12, 16), (50, 'fin_sum', 2), (51, 'fin_rec', 2), (51, 'fin_fg', 2), (51, 'scale', 2, 0, 's'), (51, 'scale', 2, 1, 'g'), (52, 'scale', 2, 2, 'g'), (52, 'scale', 2, 3, 'g'), (52, 'store', 2, 0, 4), (53, 'scale', 2, 4, 'g'), (54, 'scale', 2, 5, 'g'), (54, 'scale', 2, 6, 's'), (55, 'scale', 2, 7, 'g'), (55, 'store', 2, 4, 8), (55, 'scale', 2, 8, 'g'), (56, 'scale', 2, 9, 'v'), (57, 'scale', 2, 10, 'g'), (57, 'scale', 2, 11, 'v'), (57, 'store', 2, 8, 12), (58, 'scale', 2, 12, 'g'), (58, 'scale', 2, 13, 'g'), (59, 'scale', 2, 14, 'v'), (60, 'scale', 2, 15, 'g'), (60, 'store', 2, 12, 16)]
+        fns = {"cast": cast, "flip_x": flip_x, "product": product, "quant_x": quant_x, "mm_h": mm_h, "copy_h": copy_h, "flip_h": flip_h, "copy_hg": copy_hg, "quant_h": quant_h, "cast_cp": cast_cp, "fin_sum": fin_sum, "fin_rec": fin_rec, "fin_fg": fin_fg, "scale": scale, "store": store}
         extras = {}
+        for item in plan:
+            extras.setdefault(item[0], []).append(item[1:])
 
-        def at(i, b, fn, *args):
-            extras.setdefault((i, b), []).append((fn, args))
-
-        at(0, 0, product, 1, 2)
-        at(0, 1, product, 1, 3)
-        at(0, 2, quant_x, 1, 0)
-        at(0, 3, quant_x, 1, 1)
-        at(0, 3, mm_h, 1)
-        at(0, 4, copy_h, 1)
-        at(0, 4, flip_h, 1)
-        at(0, 5, copy_hg, 1)
-        at(0, 6, quant_h, 1)
-        at(0, 8, flip_x, 2, 0)
-        at(0, 10, product, 2, 0)
-        at(0, 12, product, 2, 1)
-        at(0, 12, flip_x, 2, 1)
-        at(0, 14, quant_x, 2, 0)
-        at(1, 0, product, 2, 2)
-        at(1, 2, product, 2, 3)
-        at(1, 3, quant_x, 2, 1)
-        at(1, 4, mm_h, 2)
-        at(1, 5, copy_h, 2)
-        at(1, 5, flip_h, 2)
-        at(1, 6, copy_hg, 2)
-        at(1, 8, quant_h, 2)
-        at(1, 8, flip_x, 3, 0)
-        at(1, 10, product, 3, 0)
-        at(1, 12, product, 3, 1)
-        at(1, 12, flip_x, 3, 1)
-        at(1, 14, quant_x, 3, 0)
-        at(2, 0, product, 3, 2)
-        at(2, 2, product, 3, 3)
-        at(2, 3, quant_x, 3, 1)
-        at(2, 4, mm_h, 3)
-        at(2, 5, copy_h, 3)
-        at(2, 5, flip_h, 3)
-        at(2, 6, copy_hg, 3)
-        at(2, 8, quant_h, 3)
-        for i in range(1, TILES):
-            at(i, 0, fin_max, i - 1)
-            at(i, 1, fin_sum, i - 1)
-            at(i, 2, fin_rec, i - 1)
-            at(i, 3, fin_fg, i - 1)
-            at(i, 3, scale_all, i - 1)
-
-        for s in range(TILES * NB):
-            reduce(s)
-            expo(s)
+        for s in range(TILES * NB + LAG):
+            if s < TILES * NB:
+                reduce(s)
+            if s > 0 and s % NB == 0:
+                fin_max(s // NB - 1)
+            if s % NB == LAG - 1 and s >= NB:
+                fin_f(s // NB - 1)
+            if s >= LAG:
+                expo(s - LAG)
             mm_l(s + LEAD)
-            for fn, args in extras.get(divmod(s, NB), []):
-                fn(*args)
+            for item in extras.get(s, []):
+                fns[item[0]](*item[1:])
 
         last = TILES - 1
-        fin_max(last)
+        for b in range(NB):
+            if SCALERS[2][b] in "VS":
+                scale(2, b, "v" if SCALERS[2][b] == "V" else "s")
+                if b % 4 == 3:
+                    store(2, b - 3, b + 1)
         fin_sum(last)
         fin_rec(last)
         fin_fg(last)
-        scale(last, 0, "v")
-        scale(last, 1, "s")
-        store(last, 0, 1)
-        store(last, 1, 2)
-        scale(last, 2, "v")
-        scale(last, 3, "v")
-        store(last, 2, 4)
-        for q in range(1, 4):
-            for b in range(4 * q, 4 * q + 4):
-                scale(last, b, "v")
-            store(last, 4 * q, 4 * q + 4)
+        for b in range(NB):
+            scale(last, b, SCALERS[last][b])
+            if b % 2 == 1:
+                store(last, b - 1, b + 1)

from contextlib import ExitStack

import concourse.mybir as mybir
from concourse.masks import make_identity

F32 = mybir.dt.float32
BF16 = mybir.dt.bfloat16
I32 = mybir.dt.int32
U32 = mybir.dt.uint32
U8 = mybir.dt.uint8
FP8 = mybir.dt.float8_e4m3fn
FP8X4 = mybir.dt.float8_e4m3fn_x4
ALU = mybir.AluOpType
ACT = mybir.ActivationFunctionType
AX = mybir.AxisListType

P = 128
TILES = 4
K1 = 2048
G1 = K1 // 512
K2 = 512
VOC = 8192
BANK = 512
NB = VOC // BANK
LAG = 2
LEAD = 5 - LAG
SCALERS = ['ggggggggsgggggsg', 'gggggggggggggggs', 'sgggggsggvgvggvg', 'vsvsvvssssvvvsvs']

FLOPS = 2 * 512 * K1 * K2 + 2 * 512 * K2 * VOC


def tile_adaptiveinputsoftmax_pa_w8_kernel(
    tc, x_bytes, x_scale, w1_words, w1_scales, w2_words, w2_scales, cluster_prob, out
):
    nc = tc.nc
    xb_hbm = x_bytes.rearrange("a b k -> (a b) k").rearrange("(p i) k -> p i k", i=TILES)
    xs_hbm = x_scale.rearrange("a b k -> (a b k)").rearrange("(g p t) -> p g t", p=P, t=4)
    cp_hbm = cluster_prob.rearrange("a b o -> (a b o)").rearrange("(p i) -> p i", i=TILES)
    out_hbm = out.rearrange("a b v -> (a b) v").rearrange("(p i) v -> p i v", i=TILES)
    w1s_hbm = w1_scales.bitcast(I32)
    w2s_hbm = w2_scales[0].bitcast(I32)
    w2w_hbm = w2_words[0].rearrange("p n t -> p (n t)").bitcast(I32)

    with ExitStack() as ctx:
        keep = ctx.enter_context(tc.tile_pool(name="keep", bufs=1))
        work = ctx.enter_context(tc.tile_pool(name="work", bufs=2))
        big = ctx.enter_context(tc.tile_pool(name="big", bufs=4))
        psum = ctx.enter_context(tc.psum_pool(name="psum", bufs=1))
        ctx.enter_context(tc.manual_schedule())

        warm = keep.tile([P, 1], F32)
        nc.vector.memset(warm[:], 0.0)
        warm_out = keep.tile([P, 1], F32)
        nc.scalar.activation(out=warm_out[:], in_=warm[:], func=ACT.Exp)
        ident = keep.tile([P, P], F32)
        make_identity(nc, ident[:])

        w1s = keep.tile([P, K2], U8, align_bytes=64)
        nc.vector.memset(w1s[:].bitcast(I32), 0)
        w2s = keep.tile([P, VOC // 4], U8, align_bytes=64)
        nc.vector.memset(w2s[:].bitcast(I32), 0)

        x8 = keep.tile([P, TILES, K1], U8, align_bytes=64)
        xs = keep.tile([P, G1, 4], F32)
        cp16 = keep.tile([P, TILES], BF16)
        w1w = keep.tile([P, G1, K2], I32, align_bytes=64)
        w2w = keep.tile([P, VOC], I32, align_bytes=64)

        def load_x(i):
            nc.sync.dma_start(out=x8[:, i, :], in_=xb_hbm[:, i, :])

        def load_w2(c):
            nc.sync.dma_start(out=w2w[:, c * 1024:(c + 1) * 1024], in_=w2w_hbm[:, c * 1024:(c + 1) * 1024])

        load_x(0)
        nc.sync.dma_start(out=xs[:], in_=xs_hbm)
        for q in range(4):
            nc.sync.dma_start(
                out=w1s[32 * q:32 * q + 16, :].bitcast(I32), in_=w1s_hbm[:, 4 * q:4 * q + 4, :]
            )
        load_x(1)
        for g in range(0, G1, 2):
            nc.sync.dma_start(
                out=w1w[:, g:g + 2, :],
                in_=w1_words[g:g + 2].rearrange("g p n t -> p g (n t)").bitcast(I32),
            )
            load_x(2 + g // 2)
        for q in range(4):
            nc.sync.dma_start(
                out=w2s[32 * q:32 * q + 16, :].bitcast(I32),
                in_=w2s_hbm[4 * q:4 * q + 4, :].rearrange("i (j c) -> j i c", j=4),
            )
        load_w2(0)
        load_w2(1)
        load_w2(2)
        nc.sync.dma_start(out=cp16[:], in_=cp_hbm)
        load_w2(3)
        for c in range(4, 8):
            load_w2(c)
        cp = keep.tile([P, TILES], F32)

        xb = [keep.tile([P, K1], BF16, name=f"xb{i}", align_bytes=64) for i in range(TILES)]
        xg = {}

        def xg_tile(i):
            if i not in xg:
                xg[i] = keep.tile([P, K1], BF16, name=f"xg{i % 2}", align_bytes=64)
            return xg[i]

        xq = [keep.tile([P, G1 * P], U32, name=f"xq{i}", align_bytes=64) for i in range(TILES)]
        xqs = [keep.tile([P, G1 * P], U8, name=f"xqs{i}", align_bytes=64) for i in range(TILES)]
        hb = [keep.tile([P, K2], BF16, name=f"hb{i}", align_bytes=64) for i in range(TILES)]
        hg = [keep.tile([P, K2], BF16, name=f"hg{i}", align_bytes=64) for i in range(TILES)]
        hq = [keep.tile([P, P], U32, name=f"hq{i}", align_bytes=64) for i in range(TILES)]
        hqs = [keep.tile([P, P], U8, name=f"hqs{i}", align_bytes=64) for i in range(TILES)]
        xt = {}
        hp = {}

        def cast(i, half, engine):
            cols = slice(half * 1024, (half + 1) * 1024)
            src = x8[:, i, cols].bitcast(FP8)
            if engine == "s":
                nc.scalar.copy(out=xb[i][:, cols], in_=src)
            elif engine == "v":
                nc.vector.tensor_copy(out=xb[i][:, cols], in_=src)
            else:
                nc.gpsimd.tensor_copy(out=xb[i][:, cols], in_=src)

        def flip_x(i, half):
            if i < 2:
                t = psum.tile([P, 4, P], F32, name="lg", bufs=5)
            else:
                t = psum.tile([P, 4, P], F32, name="xt", bufs=2)
            words = xb[i][:].bitcast(F32)
            for j in range(4):
                g = 2 * half + j // 2
                u = j % 2
                nc.tensor.transpose(t[:, j, :], words[:, 256 * g + u:256 * (g + 1):2], ident[:])
            xt[i, half] = t

        def product(i, g):
            t = xt[i, g // 2]
            j = 2 * (g % 2)
            src = t[:, j:j + 2, :].bitcast(BF16).rearrange("p u (r e) -> p r u e", e=2)
            dst = xg_tile(i)[:, 512 * g:512 * (g + 1)].rearrange("p (r u e) -> p r u e", u=2, e=2)
            sc = xs[:, g, :].rearrange("p (u e) -> p u e", e=2).unsqueeze(1).to_broadcast([P, P, 2, 2])
            nc.vector.tensor_tensor(out=dst, in0=src, in1=sc, op=ALU.mult)

        def quant_x(i):
            nc.vector.quantize_mx(out=xq[i][:].bitcast(FP8X4), scales=xqs[i][:], in_=xg_tile(i)[:])

        def mm_h(i):
            t = psum.tile([P, K2], F32, name="hp", bufs=1)
            for g in range(G1):
                nc.tensor.matmul_mx(
                    out=t[:],
                    lhsT=xq[i][:, P * g:P * (g + 1)].bitcast(FP8X4),
                    lhsT_scale=xqs[i][:, P * g:P * (g + 1)],
                    rhs=w1w[:, g, :].bitcast(FP8X4),
                    rhs_scale=w1s[4 * g:P, :],
                    start=(g == 0),
                    stop=(g == G1 - 1),
                )
            hp[i] = t

        def copy_h(i, engine="s"):
            if engine == "s":
                nc.scalar.copy(out=hb[i][:], in_=hp[i][:])
            else:
                nc.vector.tensor_copy(out=hb[i][:], in_=hp[i][:])

        def flip_h(i):
            t = psum.tile([P, 2, P], F32, name="xt", bufs=2)
            words = hb[i][:].bitcast(F32)
            for u in range(2):
                nc.tensor.transpose(t[:, u, :], words[:, u::2], ident[:])
            xt[i, "h"] = t

        def copy_hg(i, engine="s"):
            dst = hg[i][:].bitcast(F32).rearrange("p (r u) -> p r u", u=2)
            src = xt[i, "h"][:].rearrange("p u r -> p r u")
            if engine == "s":
                nc.scalar.copy(out=dst, in_=src)
            else:
                nc.vector.tensor_copy(out=dst, in_=src)

        def quant_h(i):
            nc.vector.quantize_mx(out=hq[i][:].bitcast(FP8X4), scales=hqs[i][:], in_=hg[i][:])

        e = {}
        nm = {}
        ss = {}
        fg = {}
        fc = {}
        lg = {}

        def mm_l(s):
            if s >= TILES * NB:
                return
            i, b = divmod(s, NB)
            t = psum.tile([P, BANK], F32, name="lg", bufs=5)
            cols = slice(b * BANK, (b + 1) * BANK)
            quarter, rest = divmod(b, 4)
            nc.tensor.matmul_mx(
                out=t[:],
                lhsT=hq[i][:].bitcast(FP8X4),
                lhsT_scale=hqs[i][:],
                rhs=w2w[:, cols].bitcast(FP8X4),
                rhs_scale=w2s[4 * quarter:P, rest * BANK:(rest + 1) * BANK],
                start=True,
                stop=True,
            )
            lg[s] = t

        def reduce(s):
            i, b = divmod(s, NB)
            if b == 0:
                nm[i] = work.tile([P, NB], F32, name="nm")
                ss[i] = work.tile([P, NB], F32, name="ss")
                e[i] = big.tile([P, VOC], F32, name="e")
            nc.vector.tensor_reduce(out=nm[i][:, b:b + 1], in_=lg[s][:], axis=AX.X, op=ALU.max, negate=True)

        def expo(s):
            i, b = divmod(s, NB)
            nc.scalar.activation(
                out=e[i][:, b * BANK:(b + 1) * BANK],
                in_=lg[s][:],
                func=ACT.Exp,
                bias=nm[i][:, b:b + 1],
                scale=1.0,
                accum_out=ss[i][:, b:b + 1],
            )

        fin = {}

        def fin_max(i):
            t = work.tile([P, 1], F32, name="negm")
            nc.vector.tensor_reduce(out=t[:], in_=nm[i][:], axis=AX.X, op=ALU.min)
            fin[i, "m"] = t

        def fin_f(i):
            t = fin[i, "m"]
            f = work.tile([P, NB], F32, name="f")
            nc.scalar.activation(out=f[:], in_=nm[i][:], func=ACT.Exp, bias=t[:], scale=-1.0)
            fin[i] = f
            fc[i] = work.tile([P, NB], F32, name="fc")
            nc.scalar.activation(out=fc[i][:], in_=f[:], func=ACT.Copy, scale=cp[:, i:i + 1])

        def fin_sum(i):
            prod = work.tile([P, NB], F32, name="prod")
            total = work.tile([P, 1], F32, name="total")
            nc.vector.scalar_tensor_tensor(
                out=prod[:], in0=fin[i][:], scalar=1.0, in1=ss[i][:], op0=ALU.mult, op1=ALU.mult,
                accum_out=total[:],
            )
            fin[i, "t"] = total

        def fin_rec(i):
            r = work.tile([P, 1], F32, name="r")
            nc.vector.reciprocal(out=r[:], in_=fin[i, "t"][:])
            fin[i, "r"] = r

        def fin_fg(i):
            if not any(c in "sSg" for c in SCALERS[i]):
                return
            fg[i] = work.tile([P, NB], F32, name="fg")
            nc.scalar.activation(out=fg[i][:], in_=fc[i][:], func=ACT.Copy, scale=fin[i, "r"][:])

        def scale(i, b, engine):
            part = e[i][:, b * BANK:(b + 1) * BANK]
            if engine == "s":
                nc.scalar.activation(out=part, in_=part, func=ACT.Copy, scale=fg[i][:, b:b + 1])
            elif engine == "g":
                nc.gpsimd.tensor_scalar(
                    out=part, in0=part, scalar1=fg[i][:, b:b + 1], scalar2=1.0, op0=ALU.mult, op1=ALU.mult
                )
            else:
                nc.vector.tensor_scalar(
                    out=part, in0=part, scalar1=fc[i][:, b:b + 1], scalar2=fin[i, "r"][:], op0=ALU.mult, op1=ALU.mult
                )

        def store(i, b0, b1):
            cols = slice(b0 * BANK, b1 * BANK)
            nc.sync.dma_start(out=out_hbm[:, i, cols], in_=e[i][:, cols])

        def cast_cp():
            nc.vector.tensor_copy(out=cp[:], in_=cp16[:])

        def scale_group(i, q):
            for b in range(4 * q, 4 * q + 4):
                scale(i, b, SCALERS[i][b])
            store(i, 4 * q, 4 * q + 4)

        cast(0, 0, "v")
        cast(0, 1, "s")
        flip_x(0, 0)
        flip_x(0, 1)
        for g in range(4):
            product(0, g)
        cast(1, 0, "s")
        cast(1, 1, "s")
        flip_x(1, 0)
        flip_x(1, 1)
        quant_x(0)
        mm_h(0)
        cast(2, 0, "s")
        cast(2, 1, "s")
        for g in range(4):
            product(1, g)
        copy_h(0)
        flip_h(0)
        copy_hg(0)
        quant_h(0)
        for s in range(LEAD):
            mm_l(s)
        plan = [(1, 'flip_x', 2, 0), (3, 'quant_x', 1), (4, 'cast', 3, 1, 's'), (4, 'product', 2, 0), (5, 'flip_x', 2, 1), (5, 'mm_h', 1), (6, 'product', 2, 2), (7, 'cast_cp'), (7, 'copy_h', 1, 's'), (7, 'product', 2, 3), (7, 'flip_h', 1), (9, 'product', 2, 1), (10, 'quant_x', 2), (10, 'copy_hg', 1, 's'), (10, 'mm_h', 2), (11, 'quant_h', 1), (12, 'cast', 3, 0, 's'), (13, 'flip_x', 3, 0), (15, 'copy_h', 2, 's'), (17, 'product', 3, 0), (18, 'fin_sum', 0), (19, 'flip_h', 2), (19, 'fin_rec', 0), (19, 'fin_fg', 0), (19, 'scale', 0, 0, 'g'), (19, 'scale', 0, 1, 'g'), (19, 'store', 0, 0, 2), (20, 'copy_hg', 2, 's'), (20, 'scale', 0, 2, 'g'), (20, 'scale', 0, 3, 'g'), (20, 'store', 0, 2, 4), (21, 'scale', 0, 4, 'g'), (22, 'scale', 0, 5, 'g'), (22, 'scale', 0, 6, 'g'), (23, 'flip_x', 3, 1), (23, 'quant_h', 2), (23, 'scale', 0, 7, 'g'), (23, 'store', 0, 4, 8), (23, 'scale', 0, 8, 's'), (24, 'scale', 0, 9, 'g'), (25, 'scale', 0, 10, 'g'), (25, 'scale', 0, 11, 'g'), (25, 'store', 0, 8, 12), (26, 'product', 3, 1), (26, 'scale', 0, 12, 'g'), (26, 'scale', 0, 13, 'g'), (27, 'product', 3, 2), (27, 'product', 3, 3), (27, 'scale', 0, 14, 's'), (28, 'scale', 0, 15, 'g'), (28, 'store', 0, 12, 16), (34, 'quant_x', 3), (34, 'mm_h', 3), (34, 'fin_sum', 1), (35, 'fin_rec', 1), (35, 'fin_fg', 1), (35, 'scale', 1, 0, 'g'), (35, 'scale', 1, 1, 'g'), (36, 'scale', 1, 2, 'g'), (36, 'scale', 1, 3, 'g'), (36, 'store', 1, 0, 4), (37, 'scale', 1, 4, 'g'), (38, 'copy_h', 3, 'v'), (38, 'scale', 1, 5, 'g'), (38, 'scale', 1, 6, 'g'), (39, 'flip_h', 3), (39, 'scale', 1, 7, 'g'), (39, 'store', 1, 4, 8), (39, 'scale', 1, 8, 'g'), (40, 'scale', 1, 9, 'g'), (41, 'scale', 1, 10, 'g'), (41, 'scale', 1, 11, 'g'), (41, 'store', 1, 8, 12), (42, 'scale', 1, 12, 'g'), (42, 'scale', 1, 13, 'g'), (43, 'copy_hg', 3, 's'), (43, 'scale', 1, 14, 'g'), (44, 'quant_h', 3), (44, 'scale', 1, 15, 's'), (44, 'store', 1, 12, 16), (50, 'fin_sum', 2), (51, 'fin_rec', 2), (51, 'fin_fg', 2), (51, 'scale', 2, 0, 's'), (51, 'scale', 2, 1, 'g'), (52, 'scale', 2, 2, 'g'), (52, 'scale', 2, 3, 'g'), (52, 'store', 2, 0, 4), (53, 'scale', 2, 4, 'g'), (54, 'scale', 2, 5, 'g'), (54, 'scale', 2, 6, 's'), (55, 'scale', 2, 7, 'g'), (55, 'store', 2, 4, 8), (55, 'scale', 2, 8, 'g'), (56, 'scale', 2, 9, 'v'), (57, 'scale', 2, 10, 'g'), (57, 'scale', 2, 11, 'v'), (57, 'store', 2, 8, 12), (58, 'scale', 2, 12, 'g'), (58, 'scale', 2, 13, 'g'), (59, 'scale', 2, 14, 'v'), (60, 'scale', 2, 15, 'g'), (60, 'store', 2, 12, 16)]
        fns = {"cast": cast, "flip_x": flip_x, "product": product, "quant_x": quant_x, "mm_h": mm_h, "copy_h": copy_h, "flip_h": flip_h, "copy_hg": copy_hg, "quant_h": quant_h, "cast_cp": cast_cp, "fin_sum": fin_sum, "fin_rec": fin_rec, "fin_fg": fin_fg, "scale": scale, "store": store}
        extras = {}
        for item in plan:
            extras.setdefault(item[0], []).append(item[1:])

        for s in range(TILES * NB + LAG):
            if s < TILES * NB:
                reduce(s)
            if s > 0 and s % NB == 0:
                fin_max(s // NB - 1)
            if s % NB == LAG - 1 and s >= NB:
                fin_f(s // NB - 1)
            if s >= LAG:
                expo(s - LAG)
            mm_l(s + LEAD)
            for item in extras.get(s, []):
                fns[item[0]](*item[1:])

        last = TILES - 1
        for b in range(NB):
            if SCALERS[2][b] in "VS":
                scale(2, b, "v" if SCALERS[2][b] == "V" else "s")
                if b % 4 == 3:
                    store(2, b - 3, b + 1)
        fin_sum(last)
        fin_rec(last)
        fin_fg(last)
        for b in range(NB):
            scale(last, b, SCALERS[last][b])
            if b % 2 == 1:
                store(last, b - 1, b + 1)
